import numpy as np
import ml_dtypes


def mxq(x, axis, fmt="e4m3"):
    dtype, down = {"e4m3": (ml_dtypes.float8_e4m3fn, 7), "e5m2": (ml_dtypes.float8_e5m2, 14)}[fmt]
    v = np.moveaxis(np.asarray(x, np.float32).astype(ml_dtypes.bfloat16).astype(np.float64), axis, -1)
    blocks = v.reshape(v.shape[:-1] + (-1, 32))
    amax = np.abs(blocks).max(-1, keepdims=True)
    byte = np.maximum(np.where(amax > 0, np.frexp(amax)[1] - 1 + 127, 0) - down, 1)
    scale = np.exp2(byte - 127.0)
    codes = (blocks / scale).astype(np.float32).astype(dtype).astype(np.float64)
    return np.moveaxis((codes * scale).reshape(v.shape), -1, axis)


WIDE = False


def mx_kscale(k):
    if not WIDE:
        return np.ones(k)
    levels = np.array([20, -20, 10, -10, 0])
    a = np.random.permutation(np.resize(levels, k // 512 * 4)).reshape(k // 512, 4)
    idx = np.arange(k)
    return np.exp2(a[idx // 512, idx % 128 // 32])


BF16 = ml_dtypes.bfloat16


def bf(x):
    return np.asarray(x, np.float32).astype(BF16)


def f64(x):
    return np.asarray(x).astype(np.float64)


E, M, K, N = 2, 1024, 2048, 1024


def setup_inputs():
    s = mx_kscale(M)[None, :, None]
    x = np.random.standard_normal((E, M, K)) * s
    weight = np.random.standard_normal((E, N, K)) * 0.02
    g = np.random.standard_normal((E, M, N)) * np.exp2(np.random.randint(-12, 1, (E, M, 1))) / s
    return {"x": bf(x), "weight": bf(weight), "grad_out": bf(g)}


def reference(x, weight, grad_out):
    xq = mxq(f64(x), 1, "e4m3")
    gq = mxq(f64(grad_out), 1, "e5m2")
    return gq.transpose(0, 2, 1) @ xq

@@ -1,0 +1,203 @@
+import concourse.mybir as mybir
+
+FLOPS = 2 * 2 * 1024 * 1024 * 2048
+BYTES = 2 * 1024 * 2048 * 2 + 2 * 1024 * 1024 * 2 + 2 * 1024 * 2048 * 4
+
+BF16 = mybir.dt.bfloat16
+F32 = mybir.dt.float32
+U32 = mybir.dt.uint32
+U8 = mybir.dt.uint8
+E4M3 = mybir.dt.float8_e4m3fn_x4
+E5M2 = mybir.dt.float8_e5m2_x4
+
+P = 128
+PACK = 4
+K_PASS = P * PACK
+E, M, K, N = 2, 1024, 2048, 1024
+PASSES = M // K_PASS
+KT = K // 512
+NT = N // P
+
+
+def tile_fp8groupedlineardeepgemm_kernel(tc, x, weight, grad_out, out):
+    nc = tc.nc
+    with tc.tile_pool(name="rawx", bufs=3) as rawx_pool, tc.tile_pool(
+        name="rawg", bufs=4
+    ) as rawg_pool, tc.tile_pool(name="grp", bufs=4) as grp_pool, tc.tile_pool(
+        name="keep", bufs=1
+    ) as keep, tc.tile_pool(name="stage", bufs=7) as stage_pool, tc.psum_pool(
+        name="acc", bufs=8
+    ) as psum, tc.manual_schedule():
+        xr = {}
+        gr = {}
+
+        def load_x(e, c):
+            rawx = rawx_pool.tile([P, PACK, K], BF16, name="rawx")
+            nc.sync.dma_start(
+                out=rawx[:],
+                in_=x[e, c * K_PASS : (c + 1) * K_PASS, :].rearrange("(p j) w -> p j w", j=PACK),
+            )
+            xr[(e, c)] = rawx
+
+        def load_g(e, c):
+            rawg = rawg_pool.tile([P, PACK, N], BF16, name="rawg")
+            nc.sync.dma_start(
+                out=rawg[:],
+                in_=grad_out[e, c * K_PASS : (c + 1) * K_PASS, :].rearrange(
+                    "(p j) w -> p j w", j=PACK
+                ),
+            )
+            gr[(e, c)] = rawg
+
+        load_g(0, 0)
+        load_g(0, 1)
+        load_x(0, 0)
+        load_x(0, 1)
+        load_x(1, 0)
+
+        xc = [keep.tile([P, PASSES, K], U32, name="xc%d" % e, align_bytes=64) for e in range(E)]
+        xs = [keep.tile([P, PASSES, K], U8, name="xs%d" % e, align_bytes=64) for e in range(E)]
+        gc = [keep.tile([P, 2, PASSES, 512], U32, name="gc%d" % e, align_bytes=64) for e in range(E)]
+        gs = [keep.tile([P, 2, PASSES, 512], U8, name="gs%d" % e, align_bytes=64) for e in range(E)]
+
+        def regroup(engine, dst, src):
+            d = dst.rearrange("p (c i) t -> p c t i", i=4)
+            s = src.rearrange("p t (c i) -> p c t i", i=4)
+            if engine == "v":
+                nc.vector.tensor_copy(out=d, in_=s)
+            else:
+                nc.scalar.copy(out=d, in_=s)
+
+        def new_grp():
+            grp = grp_pool.tile([P, 1024, PACK], BF16, name="grp", align_bytes=64)
+            return grp
+
+        def quant(codes, scales, grouped, fmt):
+            nc.vector.quantize_mx(
+                out=codes.bitcast(fmt),
+                scales=scales,
+                in_=grouped.rearrange("p w j -> p (w j)"),
+            )
+
+        def quant_g(e, h, grp):
+            quant(
+                gc[e][:, h, :, :].rearrange("p c w -> p (c w)"),
+                gs[e][:, h, :, :].rearrange("p c w -> p (c w)"),
+                grp[:],
+                E5M2,
+            )
+
+        def mm(acc, e, i, kt, c):
+            h, j = divmod(i, 4)
+            nc.tensor.matmul_mx(
+                out=acc[:],
+                lhsT=gc[e][:, h, c, j * P : (j + 1) * P].bitcast(E5M2),
+                lhsT_scale=gs[e][:, h, c, j * P : (j + 1) * P],
+                rhs=xc[e][:, c, kt * 512 : (kt + 1) * 512].bitcast(E4M3),
+                rhs_scale=xs[e][:, c, kt * 512 : (kt + 1) * 512],
+                start=(c == 0),
+                stop=(c == PASSES - 1),
+            )
+
+        def evac(engine, stg, kt, acc):
+            if engine == "v":
+                nc.vector.tensor_copy(out=stg[:, kt * 512 : (kt + 1) * 512], in_=acc[:])
+            else:
+                nc.scalar.copy(out=stg[:, kt * 512 : (kt + 1) * 512], in_=acc[:])
+
+        def store(e, i, stg):
+            nc.sync.dma_start(out=out[e, i * P : (i + 1) * P, :], in_=stg[:])
+
+        g_lo = new_grp()
+        g_hi = new_grp()
+        for c in range(PASSES):
+            regroup("v", g_lo[:, c * 512 : (c + 1) * 512, :], gr[(0, c)][:, :, 0:512])
+            regroup("s", g_hi[:, c * 512 : (c + 1) * 512, :], gr[(0, c)][:, :, 512:1024])
+        quant_g(0, 0, g_lo)
+        quant_g(0, 1, g_hi)
+        for c in range(PASSES):
+            xa = new_grp()
+            xb = new_grp()
+            for q in range(2):
+                regroup("v", xa[:, q * 512 : (q + 1) * 512, :], xr[(0, c)][:, :, q * 512 : (q + 1) * 512])
+                regroup(
+                    "s",
+                    xb[:, q * 512 : (q + 1) * 512, :],
+                    xr[(0, c)][:, :, 1024 + q * 512 : 1024 + (q + 1) * 512],
+                )
+            for kt in range(KT):
+                src = (xa, xb)[kt // 2]
+                q = kt % 2
+                quant(
+                    xc[0][:, c, kt * 512 : (kt + 1) * 512],
+                    xs[0][:, c, kt * 512 : (kt + 1) * 512],
+                    src[:, q * 512 : (q + 1) * 512, :],
+                    E4M3,
+                )
+            if c == 0:
+                load_x(1, 1)
+                load_g(1, 0)
+                load_g(1, 1)
+
+        accs = {}
+        stgs = {}
+        for i in range(2):
+            stgs[i] = stage_pool.tile([P, K], F32, name="stg")
+        for kt in range(KT):
+            for i in range(2):
+                accs[(i, kt)] = psum.tile([P, 512], F32, name="acc")
+                mm(accs[(i, kt)], 0, i, kt, 0)
+        for kt in range(KT):
+            for i in range(2):
+                mm(accs[(i, kt)], 0, i, kt, 1)
+        for kt in range(KT):
+            for i in range(2):
+                evac("s", stgs[i], kt, accs[(i, kt)])
+        for i in range(2):
+            store(0, i, stgs[i])
+
+        def row_tile(e, i, engines):
+            stg = stage_pool.tile([P, K], F32, name="stg")
+            for kt in range(KT):
+                acc = psum.tile([P, 512], F32, name="acc")
+                for c in range(PASSES):
+                    mm(acc, e, i, kt, c)
+                evac(engines[kt], stg, kt, acc)
+            store(e, i, stg)
+
+        for i in range(2, NT):
+            row_tile(0, i, "ssss")
+
+        tiles = []
+        for c in range(PASSES):
+            for hh in range(2):
+                tiles.append((c, hh))
+        prev = None
+        for c, hh in tiles:
+            grp = new_grp()
+            regroup("v", grp[:], xr[(1, c)][:, :, hh * 1024 : (hh + 1) * 1024])
+            if prev is not None:
+                quant(
+                    xc[1][:, prev[0], prev[1] * 1024 : (prev[1] + 1) * 1024],
+                    xs[1][:, prev[0], prev[1] * 1024 : (prev[1] + 1) * 1024],
+                    prev[2][:],
+                    E4M3,
+                )
+            prev = (c, hh, grp)
+        g_lo = new_grp()
+        for c in range(PASSES):
+            regroup("v", g_lo[:, c * 512 : (c + 1) * 512, :], gr[(1, c)][:, :, 0:512])
+        quant(
+            xc[1][:, prev[0], prev[1] * 1024 : (prev[1] + 1) * 1024],
+            xs[1][:, prev[0], prev[1] * 1024 : (prev[1] + 1) * 1024],
+            prev[2][:],
+            E4M3,
+        )
+        quant_g(1, 0, g_lo)
+        g_hi = new_grp()
+        for c in range(PASSES):
+            regroup("v", g_hi[:, c * 512 : (c + 1) * 512, :], gr[(1, c)][:, :, 512:1024])
+        quant_g(1, 1, g_hi)
+
+        for i in range(NT):
+            row_tile(1, i, "ssss" if i < 2 else "svsv")

@@ -23,9 +23,9 @@ def tile_fp8groupedlineardeepgemm_kernel(tc, x, weight, grad_out, out):
     nc = tc.nc
     with tc.tile_pool(name="rawx", bufs=3) as rawx_pool, tc.tile_pool(
         name="rawg", bufs=4
-    ) as rawg_pool, tc.tile_pool(name="grp", bufs=4) as grp_pool, tc.tile_pool(
+    ) as rawg_pool, tc.tile_pool(name="grp", bufs=3) as grp_pool, tc.tile_pool(
         name="keep", bufs=1
-    ) as keep, tc.tile_pool(name="stage", bufs=7) as stage_pool, tc.psum_pool(
+    ) as keep, tc.tile_pool(name="stage", bufs=4) as stage_pool, tc.psum_pool(
         name="acc", bufs=8
     ) as psum, tc.manual_schedule():
         xr = {}
@@ -68,6 +68,19 @@ def tile_fp8groupedlineardeepgemm_kernel(tc, x, weight, grad_out, out):
             else:
                 nc.scalar.copy(out=d, in_=s)
 
+        def regroup_g(engine, grp, e, c, h):
+            for qq in range(2):
+                d = grp[:, c * 512 + qq * 256 : c * 512 + (qq + 1) * 256, :].rearrange(
+                    "p (r a) t -> p a r t", r=2
+                )
+                s = gr[(e, c)][:, :, h * 512 + qq * 256 : h * 512 + (qq + 1) * 256].rearrange(
+                    "p t (a r) -> p a r t", r=2
+                )
+                if engine == "v":
+                    nc.vector.tensor_copy(out=d, in_=s)
+                else:
+                    nc.scalar.copy(out=d, in_=s)
+
         def new_grp():
             grp = grp_pool.tile([P, 1024, PACK], BF16, name="grp", align_bytes=64)
             return grp
@@ -99,20 +112,20 @@ def tile_fp8groupedlineardeepgemm_kernel(tc, x, weight, grad_out, out):
                 stop=(c == PASSES - 1),
             )
 
-        def evac(engine, stg, kt, acc):
+        def evac(engine, stg, r, kt, acc):
             if engine == "v":
-                nc.vector.tensor_copy(out=stg[:, kt * 512 : (kt + 1) * 512], in_=acc[:])
+                nc.vector.tensor_copy(out=stg[:, r, kt * 512 : (kt + 1) * 512], in_=acc[:])
             else:
-                nc.scalar.copy(out=stg[:, kt * 512 : (kt + 1) * 512], in_=acc[:])
+                nc.scalar.copy(out=stg[:, r, kt * 512 : (kt + 1) * 512], in_=acc[:])
 
-        def store(e, i, stg):
-            nc.sync.dma_start(out=out[e, i * P : (i + 1) * P, :], in_=stg[:])
+        def out_pair(e, q):
+            return out[e, q * 256 : (q + 1) * 256, :].rearrange("(a r) k -> a r k", r=2)
 
         g_lo = new_grp()
         g_hi = new_grp()
         for c in range(PASSES):
-            regroup("v", g_lo[:, c * 512 : (c + 1) * 512, :], gr[(0, c)][:, :, 0:512])
-            regroup("s", g_hi[:, c * 512 : (c + 1) * 512, :], gr[(0, c)][:, :, 512:1024])
+            regroup_g("v", g_lo, 0, c, 0)
+            regroup_g("s", g_hi, 0, c, 1)
         quant_g(0, 0, g_lo)
         quant_g(0, 1, g_hi)
         for c in range(PASSES):
@@ -140,33 +153,34 @@ def tile_fp8groupedlineardeepgemm_kernel(tc, x, weight, grad_out, out):
                 load_g(1, 1)
 
         accs = {}
-        stgs = {}
-        for i in range(2):
-            stgs[i] = stage_pool.tile([P, K], F32, name="stg")
+        stg0 = stage_pool.tile([P, 2, K], F32, name="stg")
         for kt in range(KT):
-            for i in range(2):
-                accs[(i, kt)] = psum.tile([P, 512], F32, name="acc")
-                mm(accs[(i, kt)], 0, i, kt, 0)
+            for r in range(2):
+                accs[(r, kt)] = psum.tile([P, 512], F32, name="acc")
+                mm(accs[(r, kt)], 0, r, kt, 0)
         for kt in range(KT):
-            for i in range(2):
-                mm(accs[(i, kt)], 0, i, kt, 1)
+            for r in range(2):
+                mm(accs[(r, kt)], 0, r, kt, 1)
         for kt in range(KT):
-            for i in range(2):
-                evac("s", stgs[i], kt, accs[(i, kt)])
-        for i in range(2):
-            store(0, i, stgs[i])
+            for r in range(2):
+                evac("s", stg0, r, kt, accs[(r, kt)])
+        nc.sync.dma_start(out=out_pair(0, 0), in_=stg0[:])
 
-        def row_tile(e, i, engines):
-            stg = stage_pool.tile([P, K], F32, name="stg")
-            for kt in range(KT):
-                acc = psum.tile([P, 512], F32, name="acc")
-                for c in range(PASSES):
-                    mm(acc, e, i, kt, c)
-                evac(engines[kt], stg, kt, acc)
-            store(e, i, stg)
+        def pair(e, q, engines, split):
+            stg = stage_pool.tile([P, 2, K], F32, name="stg")
+            for r in range(2):
+                for kt in range(KT):
+                    acc = psum.tile([P, 512], F32, name="acc")
+                    for c in range(PASSES):
+                        mm(acc, e, 2 * q + r, kt, c)
+                    evac(engines[kt], stg, r, kt, acc)
+                if split:
+                    nc.sync.dma_start(out=out_pair(e, q)[:, r, :], in_=stg[:, r, :])
+            if not split:
+                nc.sync.dma_start(out=out_pair(e, q), in_=stg[:])
 
-        for i in range(2, NT):
-            row_tile(0, i, "ssss")
+        for q in range(1, 4):
+            pair(0, q, "ssss", False)
 
         tiles = []
         for c in range(PASSES):
@@ -186,7 +200,7 @@ def tile_fp8groupedlineardeepgemm_kernel(tc, x, weight, grad_out, out):
             prev = (c, hh, grp)
         g_lo = new_grp()
         for c in range(PASSES):
-            regroup("v", g_lo[:, c * 512 : (c + 1) * 512, :], gr[(1, c)][:, :, 0:512])
+            regroup_g("v", g_lo, 1, c, 0)
         quant(
             xc[1][:, prev[0], prev[1] * 1024 : (prev[1] + 1) * 1024],
             xs[1][:, prev[0], prev[1] * 1024 : (prev[1] + 1) * 1024],
@@ -196,8 +210,8 @@ def tile_fp8groupedlineardeepgemm_kernel(tc, x, weight, grad_out, out):
         quant_g(1, 0, g_lo)
         g_hi = new_grp()
         for c in range(PASSES):
-            regroup("v", g_hi[:, c * 512 : (c + 1) * 512, :], gr[(1, c)][:, :, 512:1024])
+            regroup_g("v", g_hi, 1, c, 1)
         quant_g(1, 1, g_hi)
 
-        for i in range(NT):
-            row_tile(1, i, "ssss" if i < 2 else "svsv")
+        for q in range(4):
+            pair(1, q, "ssss" if q < 1 else "svsv", q == 3)

@@ -57,8 +57,8 @@ def tile_fp8groupedlineardeepgemm_kernel(tc, x, weight, grad_out, out):
 
         xc = [keep.tile([P, PASSES, K], U32, name="xc%d" % e, align_bytes=64) for e in range(E)]
         xs = [keep.tile([P, PASSES, K], U8, name="xs%d" % e, align_bytes=64) for e in range(E)]
-        gc = [keep.tile([P, 2, PASSES, 512], U32, name="gc%d" % e, align_bytes=64) for e in range(E)]
-        gs = [keep.tile([P, 2, PASSES, 512], U8, name="gs%d" % e, align_bytes=64) for e in range(E)]
+        gc = [keep.tile([P, 4, PASSES, 256], U32, name="gc%d" % e, align_bytes=64) for e in range(E)]
+        gs = [keep.tile([P, 4, PASSES, 256], U8, name="gs%d" % e, align_bytes=64) for e in range(E)]
 
         def regroup(engine, dst, src):
             d = dst.rearrange("p (c i) t -> p c t i", i=4)
@@ -68,18 +68,15 @@ def tile_fp8groupedlineardeepgemm_kernel(tc, x, weight, grad_out, out):
             else:
                 nc.scalar.copy(out=d, in_=s)
 
-        def regroup_g(engine, grp, e, c, h):
-            for qq in range(2):
-                d = grp[:, c * 512 + qq * 256 : c * 512 + (qq + 1) * 256, :].rearrange(
-                    "p (r a) t -> p a r t", r=2
-                )
-                s = gr[(e, c)][:, :, h * 512 + qq * 256 : h * 512 + (qq + 1) * 256].rearrange(
-                    "p t (a r) -> p a r t", r=2
-                )
-                if engine == "v":
-                    nc.vector.tensor_copy(out=d, in_=s)
-                else:
-                    nc.scalar.copy(out=d, in_=s)
+        def regroup_g(engine, grp, slot, e, c, q):
+            d = grp[:, (slot * 2 + c) * 256 : (slot * 2 + c + 1) * 256, :].rearrange(
+                "p (r a) t -> p a r t", r=2
+            )
+            s = gr[(e, c)][:, :, q * 256 : (q + 1) * 256].rearrange("p t (a r) -> p a r t", r=2)
+            if engine == "v":
+                nc.vector.tensor_copy(out=d, in_=s)
+            else:
+                nc.scalar.copy(out=d, in_=s)
 
         def new_grp():
             grp = grp_pool.tile([P, 1024, PACK], BF16, name="grp", align_bytes=64)
@@ -92,20 +89,26 @@ def tile_fp8groupedlineardeepgemm_kernel(tc, x, weight, grad_out, out):
                 in_=grouped.rearrange("p w j -> p (w j)"),
             )
 
-        def quant_g(e, h, grp):
+        def quant_g(e, q0, nq, grp):
             quant(
-                gc[e][:, h, :, :].rearrange("p c w -> p (c w)"),
-                gs[e][:, h, :, :].rearrange("p c w -> p (c w)"),
-                grp[:],
+                gc[e][:, q0 : q0 + nq, :, :].rearrange("p q c w -> p (q c w)"),
+                gs[e][:, q0 : q0 + nq, :, :].rearrange("p q c w -> p (q c w)"),
+                grp[:, 0 : nq * 512, :],
                 E5M2,
             )
 
+        def prep_g1(q):
+            grp = new_grp()
+            for c in range(PASSES):
+                regroup_g("v", grp, 0, 1, c, q)
+            return grp
+
         def mm(acc, e, i, kt, c):
-            h, j = divmod(i, 4)
+            q, r = divmod(i, 2)
             nc.tensor.matmul_mx(
                 out=acc[:],
-                lhsT=gc[e][:, h, c, j * P : (j + 1) * P].bitcast(E5M2),
-                lhsT_scale=gs[e][:, h, c, j * P : (j + 1) * P],
+                lhsT=gc[e][:, q, c, r * P : (r + 1) * P].bitcast(E5M2),
+                lhsT_scale=gs[e][:, q, c, r * P : (r + 1) * P],
                 rhs=xc[e][:, c, kt * 512 : (kt + 1) * 512].bitcast(E4M3),
                 rhs_scale=xs[e][:, c, kt * 512 : (kt + 1) * 512],
                 start=(c == 0),
@@ -124,10 +127,11 @@ def tile_fp8groupedlineardeepgemm_kernel(tc, x, weight, grad_out, out):
         g_lo = new_grp()
         g_hi = new_grp()
         for c in range(PASSES):
-            regroup_g("v", g_lo, 0, c, 0)
-            regroup_g("s", g_hi, 0, c, 1)
-        quant_g(0, 0, g_lo)
-        quant_g(0, 1, g_hi)
+            for qq in range(2):
+                regroup_g("v", g_lo, qq, 0, c, qq)
+                regroup_g("s", g_hi, qq, 0, c, 2 + qq)
+        quant_g(0, 0, 2, g_lo)
+        quant_g(0, 2, 2, g_hi)
         for c in range(PASSES):
             xa = new_grp()
             xb = new_grp()
@@ -173,14 +177,14 @@ def tile_fp8groupedlineardeepgemm_kernel(tc, x, weight, grad_out, out):
                     acc = psum.tile([P, 512], F32, name="acc")
                     for c in range(PASSES):
                         mm(acc, e, 2 * q + r, kt, c)
-                    evac(engines[kt], stg, r, kt, acc)
+                    evac(engines[r][kt], stg, r, kt, acc)
                 if split:
                     nc.sync.dma_start(out=out_pair(e, q)[:, r, :], in_=stg[:, r, :])
             if not split:
                 nc.sync.dma_start(out=out_pair(e, q), in_=stg[:])
 
-        for q in range(1, 4):
-            pair(0, q, "ssss", False)
+        for q in range(1, 3):
+            pair(0, q, ("ssss", "ssss"), False)
 
         tiles = []
         for c in range(PASSES):
@@ -198,20 +202,18 @@ def tile_fp8groupedlineardeepgemm_kernel(tc, x, weight, grad_out, out):
                     E4M3,
                 )
             prev = (c, hh, grp)
-        g_lo = new_grp()
-        for c in range(PASSES):
-            regroup_g("v", g_lo, 1, c, 0)
+        g_q = prep_g1(0)
         quant(
             xc[1][:, prev[0], prev[1] * 1024 : (prev[1] + 1) * 1024],
             xs[1][:, prev[0], prev[1] * 1024 : (prev[1] + 1) * 1024],
             prev[2][:],
             E4M3,
         )
-        quant_g(1, 0, g_lo)
-        g_hi = new_grp()
-        for c in range(PASSES):
-            regroup_g("v", g_hi, 1, c, 1)
-        quant_g(1, 1, g_hi)
+        quant_g(1, 0, 1, g_q)
 
+        pair(0, 3, ("ssss", "svsv"), False)
         for q in range(4):
-            pair(1, q, "ssss" if q < 1 else "svsv", q == 3)
+            if q + 1 < 4:
+                g_q = prep_g1(q + 1)
+                quant_g(1, q + 1, 1, g_q)
+            pair(1, q, ("svsv", "svsv"), q == 3)

@@ -25,7 +25,7 @@ def tile_fp8groupedlineardeepgemm_kernel(tc, x, weight, grad_out, out):
         name="rawg", bufs=4
     ) as rawg_pool, tc.tile_pool(name="grp", bufs=3) as grp_pool, tc.tile_pool(
         name="keep", bufs=1
-    ) as keep, tc.tile_pool(name="stage", bufs=4) as stage_pool, tc.psum_pool(
+    ) as keep, tc.tile_pool(name="stage", bufs=8) as stage_pool, tc.psum_pool(
         name="acc", bufs=8
     ) as psum, tc.manual_schedule():
         xr = {}
@@ -69,14 +69,11 @@ def tile_fp8groupedlineardeepgemm_kernel(tc, x, weight, grad_out, out):
                 nc.scalar.copy(out=d, in_=s)
 
         def regroup_g(engine, grp, slot, e, c, q):
-            d = grp[:, (slot * 2 + c) * 256 : (slot * 2 + c + 1) * 256, :].rearrange(
-                "p (r a) t -> p a r t", r=2
+            regroup(
+                engine,
+                grp[:, (slot * 2 + c) * 256 : (slot * 2 + c + 1) * 256, :],
+                gr[(e, c)][:, :, q * 256 : (q + 1) * 256],
             )
-            s = gr[(e, c)][:, :, q * 256 : (q + 1) * 256].rearrange("p t (a r) -> p a r t", r=2)
-            if engine == "v":
-                nc.vector.tensor_copy(out=d, in_=s)
-            else:
-                nc.scalar.copy(out=d, in_=s)
 
         def new_grp():
             grp = grp_pool.tile([P, 1024, PACK], BF16, name="grp", align_bytes=64)
@@ -115,14 +112,14 @@ def tile_fp8groupedlineardeepgemm_kernel(tc, x, weight, grad_out, out):
                 stop=(c == PASSES - 1),
             )
 
-        def evac(engine, stg, r, kt, acc):
+        def evac(engine, stg, kt, acc):
             if engine == "v":
-                nc.vector.tensor_copy(out=stg[:, r, kt * 512 : (kt + 1) * 512], in_=acc[:])
+                nc.vector.tensor_copy(out=stg[:, kt * 512 : (kt + 1) * 512], in_=acc[:])
             else:
-                nc.scalar.copy(out=stg[:, r, kt * 512 : (kt + 1) * 512], in_=acc[:])
+                nc.scalar.copy(out=stg[:, kt * 512 : (kt + 1) * 512], in_=acc[:])
 
-        def out_pair(e, q):
-            return out[e, q * 256 : (q + 1) * 256, :].rearrange("(a r) k -> a r k", r=2)
+        def store(e, i, stg):
+            nc.sync.dma_start(out=out[e, i * P : (i + 1) * P, :], in_=stg[:])
 
         g_lo = new_grp()
         g_hi = new_grp()
@@ -157,34 +154,32 @@ def tile_fp8groupedlineardeepgemm_kernel(tc, x, weight, grad_out, out):
                 load_g(1, 1)
 
         accs = {}
-        stg0 = stage_pool.tile([P, 2, K], F32, name="stg")
+        for r in range(2):
+            for kt in range(KT):
+                accs[(r, kt)] = psum.tile([P, 512], F32, name="acc")
         for kt in range(KT):
             for r in range(2):
-                accs[(r, kt)] = psum.tile([P, 512], F32, name="acc")
                 mm(accs[(r, kt)], 0, r, kt, 0)
         for kt in range(KT):
             for r in range(2):
                 mm(accs[(r, kt)], 0, r, kt, 1)
-        for kt in range(KT):
-            for r in range(2):
-                evac("s", stg0, r, kt, accs[(r, kt)])
-        nc.sync.dma_start(out=out_pair(0, 0), in_=stg0[:])
+        for r in range(2):
+            stg = stage_pool.tile([P, K], F32, name="stg")
+            for kt in range(KT):
+                evac("s", stg, kt, accs[(r, kt)])
+            store(0, r, stg)
 
-        def pair(e, q, engines, split):
-            stg = stage_pool.tile([P, 2, K], F32, name="stg")
-            for r in range(2):
-                for kt in range(KT):
-                    acc = psum.tile([P, 512], F32, name="acc")
-                    for c in range(PASSES):
-                        mm(acc, e, 2 * q + r, kt, c)
-                    evac(engines[r][kt], stg, r, kt, acc)
-                if split:
-                    nc.sync.dma_start(out=out_pair(e, q)[:, r, :], in_=stg[:, r, :])
-            if not split:
-                nc.sync.dma_start(out=out_pair(e, q), in_=stg[:])
+        def row_tile(e, i, engines):
+            stg = stage_pool.tile([P, K], F32, name="stg")
+            for kt in range(KT):
+                acc = psum.tile([P, 512], F32, name="acc")
+                for c in range(PASSES):
+                    mm(acc, e, i, kt, c)
+                evac(engines[kt], stg, kt, acc)
+            store(e, i, stg)
 
-        for q in range(1, 3):
-            pair(0, q, ("ssss", "ssss"), False)
+        for i in range(2, 6):
+            row_tile(0, i, "ssss")
 
         tiles = []
         for c in range(PASSES):
@@ -211,9 +206,11 @@ def tile_fp8groupedlineardeepgemm_kernel(tc, x, weight, grad_out, out):
         )
         quant_g(1, 0, 1, g_q)
 
-        pair(0, 3, ("ssss", "svsv"), False)
+        row_tile(0, 6, "ssss")
+        row_tile(0, 7, "svsv")
         for q in range(4):
             if q + 1 < 4:
                 g_q = prep_g1(q + 1)
                 quant_g(1, q + 1, 1, g_q)
-            pair(1, q, ("svsv", "svsv"), q == 3)
+            row_tile(1, 2 * q, "svsv")
+            row_tile(1, 2 * q + 1, "svsv")

import concourse.mybir as mybir

FLOPS = 2 * 2 * 1024 * 1024 * 2048
BYTES = 2 * 1024 * 2048 * 2 + 2 * 1024 * 1024 * 2 + 2 * 1024 * 2048 * 4

BF16 = mybir.dt.bfloat16
F32 = mybir.dt.float32
U32 = mybir.dt.uint32
U8 = mybir.dt.uint8
E4M3 = mybir.dt.float8_e4m3fn_x4
E5M2 = mybir.dt.float8_e5m2_x4

P = 128
PACK = 4
K_PASS = P * PACK
E, M, K, N = 2, 1024, 2048, 1024
PASSES = M // K_PASS
KT = K // 512
NT = N // P


def tile_fp8groupedlineardeepgemm_kernel(tc, x, weight, grad_out, out):
    nc = tc.nc
    with tc.tile_pool(name="rawx", bufs=3) as rawx_pool, tc.tile_pool(
        name="rawg", bufs=4
    ) as rawg_pool, tc.tile_pool(name="grp", bufs=3) as grp_pool, tc.tile_pool(
        name="keep", bufs=1
    ) as keep, tc.tile_pool(name="stage", bufs=8) as stage_pool, tc.psum_pool(
        name="acc", bufs=8
    ) as psum, tc.manual_schedule():
        xr = {}
        gr = {}

        def load_x(e, c):
            rawx = rawx_pool.tile([P, PACK, K], BF16, name="rawx")
            nc.sync.dma_start(
                out=rawx[:],
                in_=x[e, c * K_PASS : (c + 1) * K_PASS, :].rearrange("(p j) w -> p j w", j=PACK),
            )
            xr[(e, c)] = rawx

        def load_g(e, c):
            rawg = rawg_pool.tile([P, PACK, N], BF16, name="rawg")
            nc.sync.dma_start(
                out=rawg[:],
                in_=grad_out[e, c * K_PASS : (c + 1) * K_PASS, :].rearrange(
                    "(p j) w -> p j w", j=PACK
                ),
            )
            gr[(e, c)] = rawg

        load_g(0, 0)
        load_g(0, 1)
        load_x(0, 0)
        load_x(0, 1)
        load_x(1, 0)

        xc = [keep.tile([P, PASSES, K], U32, name="xc%d" % e, align_bytes=64) for e in range(E)]
        xs = [keep.tile([P, PASSES, K], U8, name="xs%d" % e, align_bytes=64) for e in range(E)]
        gc = [keep.tile([P, 4, PASSES, 256], U32, name="gc%d" % e, align_bytes=64) for e in range(E)]
        gs = [keep.tile([P, 4, PASSES, 256], U8, name="gs%d" % e, align_bytes=64) for e in range(E)]

        def regroup(engine, dst, src):
            d = dst.rearrange("p (c i) t -> p c t i", i=4)
            s = src.rearrange("p t (c i) -> p c t i", i=4)
            if engine == "v":
                nc.vector.tensor_copy(out=d, in_=s)
            else:
                nc.scalar.copy(out=d, in_=s)

        def regroup_g(engine, grp, slot, e, c, q):
            regroup(
                engine,
                grp[:, (slot * 2 + c) * 256 : (slot * 2 + c + 1) * 256, :],
                gr[(e, c)][:, :, q * 256 : (q + 1) * 256],
            )

        def new_grp():
            grp = grp_pool.tile([P, 1024, PACK], BF16, name="grp", align_bytes=64)
            return grp

        def quant(codes, scales, grouped, fmt):
            nc.vector.quantize_mx(
                out=codes.bitcast(fmt),
                scales=scales,
                in_=grouped.rearrange("p w j -> p (w j)"),
            )

        def quant_g(e, q0, nq, grp):
            quant(
                gc[e][:, q0 : q0 + nq, :, :].rearrange("p q c w -> p (q c w)"),
                gs[e][:, q0 : q0 + nq, :, :].rearrange("p q c w -> p (q c w)"),
                grp[:, 0 : nq * 512, :],
                E5M2,
            )

        def prep_g1(q):
            grp = new_grp()
            for c in range(PASSES):
                regroup_g("v", grp, 0, 1, c, q)
            return grp

        def mm(acc, e, i, kt, c):
            q, r = divmod(i, 2)
            nc.tensor.matmul_mx(
                out=acc[:],
                lhsT=gc[e][:, q, c, r * P : (r + 1) * P].bitcast(E5M2),
                lhsT_scale=gs[e][:, q, c, r * P : (r + 1) * P],
                rhs=xc[e][:, c, kt * 512 : (kt + 1) * 512].bitcast(E4M3),
                rhs_scale=xs[e][:, c, kt * 512 : (kt + 1) * 512],
                start=(c == 0),
                stop=(c == PASSES - 1),
            )

        def evac(engine, stg, kt, acc):
            if engine == "v":
                nc.vector.tensor_copy(out=stg[:, kt * 512 : (kt + 1) * 512], in_=acc[:])
            else:
                nc.scalar.copy(out=stg[:, kt * 512 : (kt + 1) * 512], in_=acc[:])

        def store(e, i, stg):
            nc.sync.dma_start(out=out[e, i * P : (i + 1) * P, :], in_=stg[:])

        g_lo = new_grp()
        g_hi = new_grp()
        for c in range(PASSES):
            for qq in range(2):
                regroup_g("v", g_lo, qq, 0, c, qq)
                regroup_g("s", g_hi, qq, 0, c, 2 + qq)
        quant_g(0, 0, 2, g_lo)
        quant_g(0, 2, 2, g_hi)
        for c in range(PASSES):
            xa = new_grp()
            xb = new_grp()
            for q in range(2):
                regroup("v", xa[:, q * 512 : (q + 1) * 512, :], xr[(0, c)][:, :, q * 512 : (q + 1) * 512])
                regroup(
                    "s",
                    xb[:, q * 512 : (q + 1) * 512, :],
                    xr[(0, c)][:, :, 1024 + q * 512 : 1024 + (q + 1) * 512],
                )
            for kt in range(KT):
                src = (xa, xb)[kt // 2]
                q = kt % 2
                quant(
                    xc[0][:, c, kt * 512 : (kt + 1) * 512],
                    xs[0][:, c, kt * 512 : (kt + 1) * 512],
                    src[:, q * 512 : (q + 1) * 512, :],
                    E4M3,
                )
            if c == 0:
                load_x(1, 1)
                load_g(1, 0)
                load_g(1, 1)

        accs = {}
        for r in range(2):
            for kt in range(KT):
                accs[(r, kt)] = psum.tile([P, 512], F32, name="acc")
        for kt in range(KT):
            for r in range(2):
                mm(accs[(r, kt)], 0, r, kt, 0)
        for kt in range(KT):
            for r in range(2):
                mm(accs[(r, kt)], 0, r, kt, 1)
        for r in range(2):
            stg = stage_pool.tile([P, K], F32, name="stg")
            for kt in range(KT):
                evac("s", stg, kt, accs[(r, kt)])
            store(0, r, stg)

        def row_tile(e, i, engines):
            stg = stage_pool.tile([P, K], F32, name="stg")
            for kt in range(KT):
                acc = psum.tile([P, 512], F32, name="acc")
                for c in range(PASSES):
                    mm(acc, e, i, kt, c)
                evac(engines[kt], stg, kt, acc)
            store(e, i, stg)

        for i in range(2, 6):
            row_tile(0, i, "ssss")

        tiles = []
        for c in range(PASSES):
            for hh in range(2):
                tiles.append((c, hh))
        prev = None
        for c, hh in tiles:
            grp = new_grp()
            regroup("v", grp[:], xr[(1, c)][:, :, hh * 1024 : (hh + 1) * 1024])
            if prev is not None:
                quant(
                    xc[1][:, prev[0], prev[1] * 1024 : (prev[1] + 1) * 1024],
                    xs[1][:, prev[0], prev[1] * 1024 : (prev[1] + 1) * 1024],
                    prev[2][:],
                    E4M3,
                )
            prev = (c, hh, grp)
        g_q = prep_g1(0)
        quant(
            xc[1][:, prev[0], prev[1] * 1024 : (prev[1] + 1) * 1024],
            xs[1][:, prev[0], prev[1] * 1024 : (prev[1] + 1) * 1024],
            prev[2][:],
            E4M3,
        )
        quant_g(1, 0, 1, g_q)

        row_tile(0, 6, "ssss")
        row_tile(0, 7, "svsv")
        for q in range(4):
            if q + 1 < 4:
                g_q = prep_g1(q + 1)
                quant_g(1, q + 1, 1, g_q)
            row_tile(1, 2 * q, "svsv")
            row_tile(1, 2 * q + 1, "svsv")
